import numpy as np
import ml_dtypes


def mxq(x, axis, fmt="e4m3"):
    dtype, down = {"e4m3": (ml_dtypes.float8_e4m3fn, 7), "e5m2": (ml_dtypes.float8_e5m2, 14)}[fmt]
    v = np.moveaxis(np.asarray(x, np.float32).astype(ml_dtypes.bfloat16).astype(np.float64), axis, -1)
    blocks = v.reshape(v.shape[:-1] + (-1, 32))
    amax = np.abs(blocks).max(-1, keepdims=True)
    byte = np.maximum(np.where(amax > 0, np.frexp(amax)[1] - 1 + 127, 0) - down, 1)
    scale = np.exp2(byte - 127.0)
    codes = (blocks / scale).astype(np.float32).astype(dtype).astype(np.float64)
    return np.moveaxis((codes * scale).reshape(v.shape), -1, axis)


WIDE = False


def mx_kscale(k):
    if not WIDE:
        return np.ones(k)
    levels = np.array([10, -10, 5, -5, 0])
    a = np.random.permutation(np.resize(levels, k // 512 * 4)).reshape(k // 512, 4)
    idx = np.arange(k)
    return np.exp2(a[idx // 512, idx % 128 // 32])


BF16 = ml_dtypes.bfloat16


def bf(x):
    return np.asarray(x, np.float32).astype(BF16)


def f64(x):
    return np.asarray(x).astype(np.float64)


B, S, D, H, KV, DH, W, KB = 4, 2048, 1024, 1, 1, 128, 128, 512
THETA = 10000.0


def rotate_half(t):
    half = t.shape[-1] // 2
    return np.concatenate((-t[..., half:], t[..., :half]), axis=-1)


def rope_cos_sin():
    inv_freq = 1.0 / THETA ** (np.arange(0, DH, 2) / DH)
    ang = np.arange(S)[:, None] * inv_freq[None, :]
    cos = np.repeat(np.cos(ang), 2, axis=-1)[None, :, None, :]
    sin = np.repeat(np.sin(ang), 2, axis=-1)[None, :, None, :]
    return cos, sin


def setup_inputs():
    s = mx_kscale(D)
    return {"x": bf(np.random.standard_normal((B, S, D)) * s),
            "Wq": bf(np.random.standard_normal((D, H * DH)) / np.sqrt(D) / s[:, None]),
            "Wk": bf(np.random.standard_normal((D, KV * DH)) / np.sqrt(D) / s[:, None]),
            "Wv": bf(np.random.standard_normal((D, KV * DH)) * 1.5 / np.sqrt(D) / s[:, None])}


def reference(x, Wq, Wk, Wv):
    cos, sin = rope_cos_sin()
    xq = mxq(f64(x), 2, "e4m3")
    q = (xq @ mxq(f64(Wq), 0, "e4m3")).reshape(B, S, H, DH)
    k = (xq @ mxq(f64(Wk), 0, "e4m3")).reshape(B, S, KV, DH)
    v = (xq @ mxq(f64(Wv), 0, "e4m3")).reshape(B, S, KV, DH)
    q = q * cos + rotate_half(q) * sin
    k = k * cos + rotate_half(k) * sin
    return q.transpose(0, 2, 1, 3), k.transpose(0, 2, 1, 3), v.transpose(0, 2, 1, 3)

@@ -1,0 +1,260 @@
+import math
+from contextlib import ExitStack
+
+import concourse.mybir as mybir
+from concourse.masks import make_identity
+
+F32 = mybir.dt.float32
+BF16 = mybir.dt.bfloat16
+I32 = mybir.dt.int32
+U32 = mybir.dt.uint32
+U8 = mybir.dt.uint8
+FP8X4 = mybir.dt.float8_e4m3fn_x4
+ALU = mybir.AluOpType
+ACT = mybir.ActivationFunctionType
+
+B, S, D, DH = 4, 2048, 1024, 128
+THETA = 10000.0
+P = 128
+J = S // P
+JN = 4
+NCH = B * J // JN
+NP = NCH * JN // 2
+NB = 8
+HALF = DH // 2
+NF = DH // 2
+NSEED = 16
+
+FLOPS = 2 * B * S * D * 3 * DH
+
+
+def tile_spikinggroupedslidingattention_pa_t_kernel(tc, x, Wq, Wk, Wv, out_0, out_1, out_2):
+    nc = tc.nc
+    chunks = [(jc, b) for jc in range(J // JN) for b in range(B)]
+    with ExitStack() as ctx:
+        const = ctx.enter_context(tc.tile_pool(name="const", bufs=1))
+        xin = ctx.enter_context(tc.tile_pool(name="xin", bufs=NB))
+        grp = ctx.enter_context(tc.tile_pool(name="grp", bufs=3))
+        cod = ctx.enter_context(tc.tile_pool(name="cod", bufs=2))
+        prod = ctx.enter_context(tc.tile_pool(name="prod", bufs=2))
+        outp = ctx.enter_context(tc.tile_pool(name="outp", bufs=3))
+        tb = ctx.enter_context(tc.tile_pool(name="tb", bufs=1))
+        ps_t = ctx.enter_context(tc.psum_pool(name="ps_t", bufs=4))
+        ps_q = ctx.enter_context(tc.psum_pool(name="ps_q", bufs=2))
+        ps_v = ctx.enter_context(tc.psum_pool(name="ps_v", bufs=2))
+        ctx.enter_context(tc.manual_schedule())
+
+        xcs = {}
+        xts = {}
+        grs = {}
+        cods = {}
+        accs = {}
+        prods = {}
+        ovs = {}
+
+        def load(c):
+            jc, b = chunks[c]
+            xc = xin.tile([P, JN * D], BF16)
+            nc.sync.dma_start(
+                out=xc[:].rearrange("p (j d) -> p j d", j=JN),
+                in_=x[b].rearrange("(p j) d -> p j d", j=J)[:, jc * JN : (jc + 1) * JN, :],
+            )
+            xcs[c] = xc
+
+        wraw = const.tile([P, 3, 2, 4, DH], BF16)
+        for wi, w_dram in enumerate((Wq, Wk, Wv)):
+            nc.scalar.dma_start(
+                out=wraw[:, wi].rearrange("p g (u e) n -> p (g u) (e n)", u=2, e=2),
+                in_=w_dram.rearrange("(a w e) n -> w a (e n)", a=4, w=P, e=2),
+            )
+        for c in range(NB):
+            load(c)
+
+        ident = const.tile([P, P], F32)
+        make_identity(nc, ident[:])
+        pos = const.tile([P, J], I32)
+        nc.gpsimd.iota(pos[:], pattern=[[1, J]], base=0, channel_multiplier=J)
+
+        ones = const.tile([P, NSEED], F32)
+        nc.vector.memset(ones[:], 1.0)
+        fq = const.tile([P, NF], F32)
+        for m in range(NSEED):
+            nc.vector.tensor_scalar_mul(
+                out=fq[:, m : m + 1], in0=ones[:, m : m + 1], scalar1=THETA ** (-m / NF) / (2.0 * math.pi)
+            )
+        n_have = NSEED
+        while n_have < NF:
+            nc.vector.tensor_scalar_mul(
+                out=fq[:, n_have : 2 * n_have], in0=fq[:, 0:n_have], scalar1=THETA ** (-n_have / NF)
+            )
+            n_have *= 2
+
+        cos_t = const.tile([P, J, DH], F32)
+        sin_t = const.tile([P, J, DH], F32)
+        tabs = {}
+
+        def table_vector(jc):
+            js = slice(jc * JN, (jc + 1) * JN)
+            turns = tb.tile([P, JN, NF], F32)
+            nc.vector.tensor_tensor(
+                out=turns[:],
+                in0=pos[:, js].unsqueeze(2).to_broadcast([P, JN, NF]),
+                in1=fq[:].unsqueeze(1).to_broadcast([P, JN, NF]),
+                op=ALU.mult,
+            )
+            whole = tb.tile([P, JN, NF], I32)
+            nc.vector.tensor_copy(out=whole[:], in_=turns[:])
+            frac = tb.tile([P, JN, NF], F32)
+            nc.vector.tensor_tensor(out=frac[:], in0=turns[:], in1=whole[:], op=ALU.subtract)
+            nabs = tb.tile([P, JN, NF], F32)
+            nc.vector.scalar_tensor_tensor(
+                out=nabs[:], in0=frac[:], scalar=-1.0, in1=frac[:], op0=ALU.mult, op1=ALU.min
+            )
+            quart = tb.tile([P, JN, NF], F32)
+            nc.vector.tensor_scalar_add(out=quart[:], in0=nabs[:], scalar1=0.25)
+            tabs[jc] = (frac, quart)
+
+        def table_scalar(jc):
+            js = slice(jc * JN, (jc + 1) * JN)
+            frac, quart = tabs[jc]
+            nc.scalar.activation(
+                out=cos_t[:, js, :].rearrange("p j (m e) -> p j m e", e=2),
+                in_=quart[:].unsqueeze(3).to_broadcast([P, JN, NF, 2]),
+                func=ACT.Sin,
+                scale=2.0 * math.pi,
+            )
+            nc.scalar.activation(
+                out=sin_t[:, js, 0:HALF].rearrange("p j (m e) -> p j m e", e=2),
+                in_=frac[:, :, NF // 2 : NF].unsqueeze(3).to_broadcast([P, JN, NF // 2, 2]),
+                func=ACT.Sin,
+                scale=2.0 * math.pi,
+            )
+            nc.scalar.activation(
+                out=sin_t[:, js, HALF:DH].rearrange("p j (m e) -> p j m e", e=2),
+                in_=frac[:, :, 0 : NF // 2].unsqueeze(3).to_broadcast([P, JN, NF // 2, 2]),
+                func=ACT.Sin,
+                scale=-2.0 * math.pi,
+            )
+
+        table_vector(0)
+
+        wg = const.tile([P, 2, 3 * DH, 4], BF16, align_bytes=64)
+        for wi in range(3):
+            nc.vector.tensor_copy(
+                out=wg[:, :, wi * DH : (wi + 1) * DH, :], in_=wraw[:, wi].rearrange("p g t n -> p g n t")
+            )
+        wcod = const.tile([P, 2, 3 * DH], U32, align_bytes=64)
+        wsc = const.tile([P, 2, 3 * DH], U8, align_bytes=64)
+        for g in range(2):
+            for c0, c1 in ((0, 2 * DH), (2 * DH, 3 * DH)):
+                nc.vector.quantize_mx(
+                    out=wcod[:, g, c0:c1].bitcast(FP8X4),
+                    scales=wsc[:, g, c0:c1],
+                    in_=wg[:, g, c0:c1, :].rearrange("p n t -> p (n t)"),
+                )
+
+        def transposes(i):
+            xw = xcs[i // 2][:].bitcast(F32)
+            tiles = []
+            for a in range(2):
+                jj = (i % 2) * 2 + a
+                xt = ps_t.tile([P, 4, P], F32)
+                for u in range(4):
+                    col = jj * (D // 2) + u * P
+                    nc.tensor.transpose(xt[:, u, :], xw[:, col : col + P], ident[:])
+                tiles.append(xt)
+            xts[i] = tiles
+
+        def regroup(i):
+            gr = grp.tile([P, 2 * D], BF16, align_bytes=64)
+            grw = gr[:].bitcast(F32)
+            for a in range(2):
+                nc.scalar.copy(
+                    out=grw[:, a * (D // 2) : (a + 1) * (D // 2)].rearrange("p (g r u) -> p g r u", g=2, r=P, u=2),
+                    in_=xts[i][a][:].rearrange("p (g u) r -> p g r u", g=2, u=2),
+                )
+            grs[i] = gr
+
+        def quantise(i):
+            xcod = cod.tile([P, D // 2], U32, align_bytes=64)
+            xsc = cod.tile([P, D // 2], U8, align_bytes=64)
+            nc.vector.quantize_mx(out=xcod[:].bitcast(FP8X4), scales=xsc[:], in_=grs[i][:])
+            cods[i] = (xcod, xsc)
+
+        def multiply(i):
+            xcod, xsc = cods[i]
+            qk = ps_q.tile([P, 4 * DH], F32)
+            vv = ps_v.tile([P, 2 * DH], F32)
+            for a in range(2):
+                for dst, c0, c1 in (
+                    (qk[:, a * 2 * DH : (a + 1) * 2 * DH], 0, 2 * DH),
+                    (vv[:, a * DH : (a + 1) * DH], 2 * DH, 3 * DH),
+                ):
+                    for g in range(2):
+                        cols = slice((a * 2 + g) * P, (a * 2 + g + 1) * P)
+                        nc.tensor.matmul_mx(
+                            out=dst,
+                            lhsT=xcod[:, cols].bitcast(FP8X4),
+                            lhsT_scale=xsc[:, cols],
+                            rhs=wcod[:, g, c0:c1].bitcast(FP8X4),
+                            rhs_scale=wsc[:, g, c0:c1],
+                            start=(g == 0),
+                            stop=(g == 1),
+                        )
+            accs[i] = (qk, vv)
+
+        def finish(i):
+            c = i // 2
+            jc, b = chunks[c]
+            jj0 = (i % 2) * 2
+            j0 = jc * JN + jj0
+            qk, vv = accs[i]
+            if i % 2 == 0:
+                pt = prod.tile([P, 2, JN, 2, DH], F32)
+                prods[c] = pt
+                ov = outp.tile([P, JN, DH], F32)
+                ovs[c] = ov
+            pt = prods[c]
+            ov = ovs[c]
+            for k, table in enumerate((cos_t, sin_t)):
+                nc.vector.tensor_tensor(
+                    out=pt[:, k, jj0 : jj0 + 2, :, :],
+                    in0=qk[:].rearrange("p (a q f) -> p a q f", a=2, q=2),
+                    in1=table[:, j0 : j0 + 2, :].unsqueeze(2).to_broadcast([P, 2, 2, DH]),
+                    op=ALU.mult,
+                )
+            nc.scalar.copy(out=ov[:, jj0 : jj0 + 2, :], in_=vv[:].rearrange("p (a f) -> p a f", a=2))
+            if i % 2 == 1:
+                oqk = outp.tile([P, 2, JN, DH], F32)
+                for h in range(2):
+                    nc.vector.tensor_tensor(
+                        out=oqk[:, :, :, h * HALF : (h + 1) * HALF],
+                        in0=pt[:, 0, :, :, h * HALF : (h + 1) * HALF].rearrange("p a q f -> p q a f"),
+                        in1=pt[:, 1, :, :, (1 - h) * HALF : (2 - h) * HALF].rearrange("p a q f -> p q a f"),
+                        op=ALU.add,
+                    )
+                js = slice(jc * JN, (jc + 1) * JN)
+                for dram, src in ((out_0, oqk[:, 0, :, :]), (out_1, oqk[:, 1, :, :]), (out_2, ov[:])):
+                    nc.sync.dma_start(out=dram[b, 0].rearrange("(p j) f -> p j f", j=J)[:, js, :], in_=src)
+
+        transposes(0)
+        regroup(0)
+        transposes(1)
+        load(NB)
+        regroup(1)
+        table_scalar(0)
+        for i in range(NP):
+            if i + 2 < NP:
+                transposes(i + 2)
+                if (i + 2) % 2 == 1 and (i + 2) // 2 + NB < NCH:
+                    load((i + 2) // 2 + NB)
+            quantise(i)
+            multiply(i)
+            if i >= 1:
+                finish(i - 1)
+            if i + 2 < NP:
+                regroup(i + 2)
+            if i % 8 == 3 and i // 8 + 1 < J // JN:
+                table_vector(i // 8 + 1)
+                table_scalar(i // 8 + 1)
+        finish(NP - 1)

@@ -20,10 +20,10 @@ J = S // P
 JN = 4
 NCH = B * J // JN
 NP = NCH * JN // 2
-NB = 8
+LEAD = 6
 HALF = DH // 2
 NF = DH // 2
-NSEED = 16
+NSEED = 8
 
 FLOPS = 2 * B * S * D * 3 * DH
 
@@ -33,11 +33,11 @@ def tile_spikinggroupedslidingattention_pa_t_kernel(tc, x, Wq, Wk, Wv, out_0, ou
     chunks = [(jc, b) for jc in range(J // JN) for b in range(B)]
     with ExitStack() as ctx:
         const = ctx.enter_context(tc.tile_pool(name="const", bufs=1))
-        xin = ctx.enter_context(tc.tile_pool(name="xin", bufs=NB))
+        xin = ctx.enter_context(tc.tile_pool(name="xin", bufs=NCH))
         grp = ctx.enter_context(tc.tile_pool(name="grp", bufs=3))
         cod = ctx.enter_context(tc.tile_pool(name="cod", bufs=2))
-        prod = ctx.enter_context(tc.tile_pool(name="prod", bufs=2))
-        outp = ctx.enter_context(tc.tile_pool(name="outp", bufs=3))
+        prod = ctx.enter_context(tc.tile_pool(name="prod", bufs=3))
+        outp = ctx.enter_context(tc.tile_pool(name="outp", bufs=4))
         tb = ctx.enter_context(tc.tile_pool(name="tb", bufs=1))
         ps_t = ctx.enter_context(tc.psum_pool(name="ps_t", bufs=4))
         ps_q = ctx.enter_context(tc.psum_pool(name="ps_q", bufs=2))
@@ -49,16 +49,18 @@ def tile_spikinggroupedslidingattention_pa_t_kernel(tc, x, Wq, Wk, Wv, out_0, ou
         grs = {}
         cods = {}
         accs = {}
-        prods = {}
+        oqks = {}
         ovs = {}
 
-        def load(c):
+        def load(c, pieces):
             jc, b = chunks[c]
             xc = xin.tile([P, JN * D], BF16)
-            nc.sync.dma_start(
-                out=xc[:].rearrange("p (j d) -> p j d", j=JN),
-                in_=x[b].rearrange("(p j) d -> p j d", j=J)[:, jc * JN : (jc + 1) * JN, :],
-            )
+            step = JN // pieces
+            for lo in range(0, JN, step):
+                nc.sync.dma_start(
+                    out=xc[:, lo * D : (lo + step) * D].rearrange("p (j d) -> p j d", j=step),
+                    in_=x[b].rearrange("(p j) d -> p j d", j=J)[:, jc * JN + lo : jc * JN + lo + step, :],
+                )
             xcs[c] = xc
 
         wraw = const.tile([P, 3, 2, 4, DH], BF16)
@@ -67,8 +69,8 @@ def tile_spikinggroupedslidingattention_pa_t_kernel(tc, x, Wq, Wk, Wv, out_0, ou
                 out=wraw[:, wi].rearrange("p g (u e) n -> p (g u) (e n)", u=2, e=2),
                 in_=w_dram.rearrange("(a w e) n -> w a (e n)", a=4, w=P, e=2),
             )
-        for c in range(NB):
-            load(c)
+        for c in range(LEAD):
+            load(c, 2 if c == 0 else 1)
 
         ident = const.tile([P, P], F32)
         make_identity(nc, ident[:])
@@ -77,6 +79,8 @@ def tile_spikinggroupedslidingattention_pa_t_kernel(tc, x, Wq, Wk, Wv, out_0, ou
 
         ones = const.tile([P, NSEED], F32)
         nc.vector.memset(ones[:], 1.0)
+        warm = const.tile([P, 1], F32)
+        nc.scalar.activation(out=warm[:], in_=ones[:, 0:1], func=ACT.Sin)
         fq = const.tile([P, NF], F32)
         for m in range(NSEED):
             nc.vector.tensor_scalar_mul(
@@ -92,6 +96,8 @@ def tile_spikinggroupedslidingattention_pa_t_kernel(tc, x, Wq, Wk, Wv, out_0, ou
         cos_t = const.tile([P, J, DH], F32)
         sin_t = const.tile([P, J, DH], F32)
         tabs = {}
+        halves = {}
+        squares = {}
 
         def table_vector(jc):
             js = slice(jc * JN, (jc + 1) * JN)
@@ -106,47 +112,60 @@ def tile_spikinggroupedslidingattention_pa_t_kernel(tc, x, Wq, Wk, Wv, out_0, ou
             nc.vector.tensor_copy(out=whole[:], in_=turns[:])
             frac = tb.tile([P, JN, NF], F32)
             nc.vector.tensor_tensor(out=frac[:], in0=turns[:], in1=whole[:], op=ALU.subtract)
-            nabs = tb.tile([P, JN, NF], F32)
-            nc.vector.scalar_tensor_tensor(
-                out=nabs[:], in0=frac[:], scalar=-1.0, in1=frac[:], op0=ALU.mult, op1=ALU.min
-            )
-            quart = tb.tile([P, JN, NF], F32)
-            nc.vector.tensor_scalar_add(out=quart[:], in0=nabs[:], scalar1=0.25)
-            tabs[jc] = (frac, quart)
+            tabs[jc] = frac
 
-        def table_scalar(jc):
+        def table_scalar(jc, part):
             js = slice(jc * JN, (jc + 1) * JN)
-            frac, quart = tabs[jc]
-            nc.scalar.activation(
-                out=cos_t[:, js, :].rearrange("p j (m e) -> p j m e", e=2),
-                in_=quart[:].unsqueeze(3).to_broadcast([P, JN, NF, 2]),
-                func=ACT.Sin,
-                scale=2.0 * math.pi,
-            )
-            nc.scalar.activation(
-                out=sin_t[:, js, 0:HALF].rearrange("p j (m e) -> p j m e", e=2),
-                in_=frac[:, :, NF // 2 : NF].unsqueeze(3).to_broadcast([P, JN, NF // 2, 2]),
-                func=ACT.Sin,
-                scale=2.0 * math.pi,
-            )
-            nc.scalar.activation(
-                out=sin_t[:, js, HALF:DH].rearrange("p j (m e) -> p j m e", e=2),
-                in_=frac[:, :, 0 : NF // 2].unsqueeze(3).to_broadcast([P, JN, NF // 2, 2]),
-                func=ACT.Sin,
-                scale=-2.0 * math.pi,
-            )
+            frac = tabs[jc]
+            if part == 0:
+                hs = tb.tile([P, JN, NF], F32)
+                nc.scalar.activation(out=hs[:], in_=frac[:], func=ACT.Sin, scale=math.pi)
+                halves[jc] = hs
+            elif part == 1:
+                sq = tb.tile([P, JN, NF], F32)
+                nc.scalar.activation(out=sq[:], in_=halves[jc][:], func=ACT.Square)
+                squares[jc] = sq
+            elif part == 2:
+                nc.scalar.activation(
+                    out=cos_t[:, js, :].rearrange("p j (m e) -> p j m e", e=2),
+                    in_=squares[jc][:].unsqueeze(3).to_broadcast([P, JN, NF, 2]),
+                    func=ACT.Copy,
+                    bias=1.0,
+                    scale=-2.0,
+                )
+            elif part == 3:
+                nc.scalar.activation(
+                    out=sin_t[:, js, 0:HALF].rearrange("p j (m e) -> p j m e", e=2),
+                    in_=frac[:, :, NF // 2 : NF].unsqueeze(3).to_broadcast([P, JN, NF // 2, 2]),
+                    func=ACT.Sin,
+                    scale=2.0 * math.pi,
+                )
+            else:
+                nc.scalar.activation(
+                    out=sin_t[:, js, HALF:DH].rearrange("p j (m e) -> p j m e", e=2),
+                    in_=frac[:, :, 0 : NF // 2].unsqueeze(3).to_broadcast([P, JN, NF // 2, 2]),
+                    func=ACT.Sin,
+                    scale=-2.0 * math.pi,
+                )
 
         table_vector(0)
+        for part in range(5):
+            table_scalar(0, part)
 
         wg = const.tile([P, 2, 3 * DH, 4], BF16, align_bytes=64)
         for wi in range(3):
-            nc.vector.tensor_copy(
-                out=wg[:, :, wi * DH : (wi + 1) * DH, :], in_=wraw[:, wi].rearrange("p g t n -> p g n t")
-            )
+            if wi < 2:
+                nc.vector.tensor_copy(
+                    out=wg[:, :, wi * DH : (wi + 1) * DH, :], in_=wraw[:, wi].rearrange("p g t n -> p g n t")
+                )
+            else:
+                nc.scalar.copy(
+                    out=wg[:, :, wi * DH : (wi + 1) * DH, :], in_=wraw[:, wi].rearrange("p g t n -> p g n t")
+                )
         wcod = const.tile([P, 2, 3 * DH], U32, align_bytes=64)
         wsc = const.tile([P, 2, 3 * DH], U8, align_bytes=64)
-        for g in range(2):
-            for c0, c1 in ((0, 2 * DH), (2 * DH, 3 * DH)):
+        for c0, c1 in ((0, 2 * DH), (2 * DH, 3 * DH)):
+            for g in range(2):
                 nc.vector.quantize_mx(
                     out=wcod[:, g, c0:c1].bitcast(FP8X4),
                     scales=wsc[:, g, c0:c1],
@@ -203,6 +222,17 @@ def tile_spikinggroupedslidingattention_pa_t_kernel(tc, x, Wq, Wk, Wv, out_0, ou
                         )
             accs[i] = (qk, vv)
 
+        def store(c, lo, hi):
+            jc, b = chunks[c]
+            js = slice(jc * JN + lo, jc * JN + hi)
+            oqk = oqks[c]
+            for dram, src in (
+                (out_0, oqk[:, 0, lo:hi, :]),
+                (out_1, oqk[:, 1, lo:hi, :]),
+                (out_2, ovs[c][:, lo:hi, :]),
+            ):
+                nc.sync.dma_start(out=dram[b, 0].rearrange("(p j) f -> p j f", j=J)[:, js, :], in_=src)
+
         def finish(i):
             c = i // 2
             jc, b = chunks[c]
@@ -210,51 +240,53 @@ def tile_spikinggroupedslidingattention_pa_t_kernel(tc, x, Wq, Wk, Wv, out_0, ou
             j0 = jc * JN + jj0
             qk, vv = accs[i]
             if i % 2 == 0:
-                pt = prod.tile([P, 2, JN, 2, DH], F32)
-                prods[c] = pt
                 ov = outp.tile([P, JN, DH], F32)
                 ovs[c] = ov
-            pt = prods[c]
+                oqk = outp.tile([P, 2, JN, DH], F32)
+                oqks[c] = oqk
             ov = ovs[c]
+            oqk = oqks[c]
+            pt = prod.tile([P, 2, 2, 2, DH], F32)
             for k, table in enumerate((cos_t, sin_t)):
                 nc.vector.tensor_tensor(
-                    out=pt[:, k, jj0 : jj0 + 2, :, :],
+                    out=pt[:, k, :, :, :],
                     in0=qk[:].rearrange("p (a q f) -> p a q f", a=2, q=2),
                     in1=table[:, j0 : j0 + 2, :].unsqueeze(2).to_broadcast([P, 2, 2, DH]),
                     op=ALU.mult,
                 )
             nc.scalar.copy(out=ov[:, jj0 : jj0 + 2, :], in_=vv[:].rearrange("p (a f) -> p a f", a=2))
-            if i % 2 == 1:
-                oqk = outp.tile([P, 2, JN, DH], F32)
-                for h in range(2):
-                    nc.vector.tensor_tensor(
-                        out=oqk[:, :, :, h * HALF : (h + 1) * HALF],
-                        in0=pt[:, 0, :, :, h * HALF : (h + 1) * HALF].rearrange("p a q f -> p q a f"),
-                        in1=pt[:, 1, :, :, (1 - h) * HALF : (2 - h) * HALF].rearrange("p a q f -> p q a f"),
-                        op=ALU.add,
-                    )
-                js = slice(jc * JN, (jc + 1) * JN)
-                for dram, src in ((out_0, oqk[:, 0, :, :]), (out_1, oqk[:, 1, :, :]), (out_2, ov[:])):
-                    nc.sync.dma_start(out=dram[b, 0].rearrange("(p j) f -> p j f", j=J)[:, js, :], in_=src)
+            for h in range(2):
+                adder = nc.vector if (i == NP - 1 and h == 0) else nc.gpsimd
+                adder.tensor_tensor(
+                    out=oqk[:, :, jj0 : jj0 + 2, h * HALF : (h + 1) * HALF],
+                    in0=pt[:, 0, :, :, h * HALF : (h + 1) * HALF].rearrange("p a q f -> p q a f"),
+                    in1=pt[:, 1, :, :, (1 - h) * HALF : (2 - h) * HALF].rearrange("p a q f -> p q a f"),
+                    op=ALU.add,
+                )
+            if c == NCH - 1:
+                store(c, jj0, jj0 + 2)
+            elif i % 2 == 1:
+                store(c, 0, JN)
+                if c + LEAD < NCH:
+                    load(c + LEAD, 1)
 
         transposes(0)
         regroup(0)
         transposes(1)
-        load(NB)
         regroup(1)
-        table_scalar(0)
         for i in range(NP):
             if i + 2 < NP:
                 transposes(i + 2)
-                if (i + 2) % 2 == 1 and (i + 2) // 2 + NB < NCH:
-                    load((i + 2) // 2 + NB)
             quantise(i)
             multiply(i)
             if i >= 1:
                 finish(i - 1)
             if i + 2 < NP:
                 regroup(i + 2)
-            if i % 8 == 3 and i // 8 + 1 < J // JN:
-                table_vector(i // 8 + 1)
-                table_scalar(i // 8 + 1)
+            nxt = i // 8 + 1
+            if nxt < J // JN:
+                if i % 8 == 2:
+                    table_vector(nxt)
+                if i % 8 >= 3:
+                    table_scalar(nxt, i % 8 - 3)
         finish(NP - 1)

@@ -20,7 +20,8 @@ J = S // P
 JN = 4
 NCH = B * J // JN
 NP = NCH * JN // 2
-LEAD = 6
+LEAD = 8
+NB = 10
 HALF = DH // 2
 NF = DH // 2
 NSEED = 8
@@ -33,10 +34,10 @@ def tile_spikinggroupedslidingattention_pa_t_kernel(tc, x, Wq, Wk, Wv, out_0, ou
     chunks = [(jc, b) for jc in range(J // JN) for b in range(B)]
     with ExitStack() as ctx:
         const = ctx.enter_context(tc.tile_pool(name="const", bufs=1))
-        xin = ctx.enter_context(tc.tile_pool(name="xin", bufs=NCH))
-        grp = ctx.enter_context(tc.tile_pool(name="grp", bufs=3))
-        cod = ctx.enter_context(tc.tile_pool(name="cod", bufs=2))
-        prod = ctx.enter_context(tc.tile_pool(name="prod", bufs=3))
+        xin = ctx.enter_context(tc.tile_pool(name="xin", bufs=NB))
+        grp = ctx.enter_context(tc.tile_pool(name="grp", bufs=4))
+        cod = ctx.enter_context(tc.tile_pool(name="cod", bufs=4))
+        prod = ctx.enter_context(tc.tile_pool(name="prod", bufs=2))
         outp = ctx.enter_context(tc.tile_pool(name="outp", bufs=4))
         tb = ctx.enter_context(tc.tile_pool(name="tb", bufs=1))
         ps_t = ctx.enter_context(tc.psum_pool(name="ps_t", bufs=4))
@@ -50,32 +51,39 @@ def tile_spikinggroupedslidingattention_pa_t_kernel(tc, x, Wq, Wk, Wv, out_0, ou
         cods = {}
         accs = {}
         oqks = {}
+        pts = {}
         ovs = {}
 
-        def load(c, pieces):
+        def load_part(c, lo, hi):
             jc, b = chunks[c]
+            nc.sync.dma_start(
+                out=xcs[c][:, lo * D : hi * D].rearrange("p (j d) -> p j d", j=hi - lo),
+                in_=x[b].rearrange("(p j) d -> p j d", j=J)[:, jc * JN + lo : jc * JN + hi, :],
+            )
+
+        def load(c):
             xc = xin.tile([P, JN * D], BF16)
-            step = JN // pieces
-            for lo in range(0, JN, step):
-                nc.sync.dma_start(
-                    out=xc[:, lo * D : (lo + step) * D].rearrange("p (j d) -> p j d", j=step),
-                    in_=x[b].rearrange("(p j) d -> p j d", j=J)[:, jc * JN + lo : jc * JN + lo + step, :],
-                )
             xcs[c] = xc
+            if c > 0:
+                load_part(c, 0, JN)
 
         wraw = const.tile([P, 3, 2, 4, DH], BF16)
+        load(0)
+        load_part(0, 0, 1)
         for wi, w_dram in enumerate((Wq, Wk, Wv)):
-            nc.scalar.dma_start(
+            nc.sync.dma_start(
                 out=wraw[:, wi].rearrange("p g (u e) n -> p (g u) (e n)", u=2, e=2),
                 in_=w_dram.rearrange("(a w e) n -> w a (e n)", a=4, w=P, e=2),
             )
-        for c in range(LEAD):
-            load(c, 2 if c == 0 else 1)
+        load_part(0, 1, 2)
+        load_part(0, 2, JN)
+        for c in range(1, LEAD):
+            load(c)
 
         ident = const.tile([P, P], F32)
         make_identity(nc, ident[:])
-        pos = const.tile([P, J], I32)
-        nc.gpsimd.iota(pos[:], pattern=[[1, J]], base=0, channel_multiplier=J)
+        pos_i = const.tile([P, J], I32)
+        nc.gpsimd.iota(pos_i[:], pattern=[[1, J]], base=0, channel_multiplier=J)
 
         ones = const.tile([P, NSEED], F32)
         nc.vector.memset(ones[:], 1.0)
@@ -92,24 +100,33 @@ def tile_spikinggroupedslidingattention_pa_t_kernel(tc, x, Wq, Wk, Wv, out_0, ou
                 out=fq[:, n_have : 2 * n_have], in0=fq[:, 0:n_have], scalar1=THETA ** (-n_have / NF)
             )
             n_have *= 2
+        pos = const.tile([P, J], F32)
+        nc.vector.tensor_copy(out=pos[:], in_=pos_i[:])
 
         cos_t = const.tile([P, J, DH], F32)
         sin_t = const.tile([P, J, DH], F32)
         tabs = {}
+        raws = {}
         halves = {}
         squares = {}
 
-        def table_vector(jc):
+        def table_gpsimd(jc):
             js = slice(jc * JN, (jc + 1) * JN)
             turns = tb.tile([P, JN, NF], F32)
-            nc.vector.tensor_tensor(
+            nc.gpsimd.tensor_tensor(
                 out=turns[:],
                 in0=pos[:, js].unsqueeze(2).to_broadcast([P, JN, NF]),
                 in1=fq[:].unsqueeze(1).to_broadcast([P, JN, NF]),
                 op=ALU.mult,
             )
             whole = tb.tile([P, JN, NF], I32)
-            nc.vector.tensor_copy(out=whole[:], in_=turns[:])
+            nc.gpsimd.tensor_scalar(
+                out=whole[:], in0=turns[:], scalar1=1.0, scalar2=0.0, op0=ALU.mult, op1=ALU.add
+            )
+            raws[jc] = (turns, whole)
+
+        def table_vector(jc):
+            turns, whole = raws[jc]
             frac = tb.tile([P, JN, NF], F32)
             nc.vector.tensor_tensor(out=frac[:], in0=turns[:], in1=whole[:], op=ALU.subtract)
             tabs[jc] = frac
@@ -148,9 +165,8 @@ def tile_spikinggroupedslidingattention_pa_t_kernel(tc, x, Wq, Wk, Wv, out_0, ou
                     scale=-2.0 * math.pi,
                 )
 
+        table_gpsimd(0)
         table_vector(0)
-        for part in range(5):
-            table_scalar(0, part)
 
         wg = const.tile([P, 2, 3 * DH, 4], BF16, align_bytes=64)
         for wi in range(3):
@@ -159,8 +175,13 @@ def tile_spikinggroupedslidingattention_pa_t_kernel(tc, x, Wq, Wk, Wv, out_0, ou
                     out=wg[:, :, wi * DH : (wi + 1) * DH, :], in_=wraw[:, wi].rearrange("p g t n -> p g n t")
                 )
             else:
-                nc.scalar.copy(
-                    out=wg[:, :, wi * DH : (wi + 1) * DH, :], in_=wraw[:, wi].rearrange("p g t n -> p g n t")
+                nc.gpsimd.tensor_scalar(
+                    out=wg[:, :, wi * DH : (wi + 1) * DH, :],
+                    in0=wraw[:, wi].rearrange("p g t n -> p g n t"),
+                    scalar1=1.0,
+                    scalar2=0.0,
+                    op0=ALU.mult,
+                    op1=ALU.add,
                 )
         wcod = const.tile([P, 2, 3 * DH], U32, align_bytes=64)
         wsc = const.tile([P, 2, 3 * DH], U8, align_bytes=64)
@@ -184,15 +205,19 @@ def tile_spikinggroupedslidingattention_pa_t_kernel(tc, x, Wq, Wk, Wv, out_0, ou
                 tiles.append(xt)
             xts[i] = tiles
 
+        def regroup_tile(i, a):
+            if a == 0:
+                gr = grp.tile([P, 2 * D], BF16, align_bytes=64)
+                grs[i] = gr
+            grw = grs[i][:].bitcast(F32)
+            nc.scalar.copy(
+                out=grw[:, a * (D // 2) : (a + 1) * (D // 2)].rearrange("p (g r u) -> p g r u", g=2, r=P, u=2),
+                in_=xts[i][a][:].rearrange("p (g u) r -> p g r u", g=2, u=2),
+            )
+
         def regroup(i):
-            gr = grp.tile([P, 2 * D], BF16, align_bytes=64)
-            grw = gr[:].bitcast(F32)
-            for a in range(2):
-                nc.scalar.copy(
-                    out=grw[:, a * (D // 2) : (a + 1) * (D // 2)].rearrange("p (g r u) -> p g r u", g=2, r=P, u=2),
-                    in_=xts[i][a][:].rearrange("p (g u) r -> p g r u", g=2, u=2),
-                )
-            grs[i] = gr
+            regroup_tile(i, 0)
+            regroup_tile(i, 1)
 
         def quantise(i):
             xcod = cod.tile([P, D // 2], U32, align_bytes=64)
@@ -233,60 +258,98 @@ def tile_spikinggroupedslidingattention_pa_t_kernel(tc, x, Wq, Wk, Wv, out_0, ou
             ):
                 nc.sync.dma_start(out=dram[b, 0].rearrange("(p j) f -> p j f", j=J)[:, js, :], in_=src)
 
-        def finish(i):
+        def products(i):
             c = i // 2
             jc, b = chunks[c]
             jj0 = (i % 2) * 2
             j0 = jc * JN + jj0
-            qk, vv = accs[i]
             if i % 2 == 0:
-                ov = outp.tile([P, JN, DH], F32)
-                ovs[c] = ov
-                oqk = outp.tile([P, 2, JN, DH], F32)
-                oqks[c] = oqk
-            ov = ovs[c]
-            oqk = oqks[c]
-            pt = prod.tile([P, 2, 2, 2, DH], F32)
+                pt = prod.tile([P, 2, JN, 2, DH], F32)
+                pts[c] = pt
             for k, table in enumerate((cos_t, sin_t)):
                 nc.vector.tensor_tensor(
-                    out=pt[:, k, :, :, :],
-                    in0=qk[:].rearrange("p (a q f) -> p a q f", a=2, q=2),
+                    out=pts[c][:, k, jj0 : jj0 + 2, :, :],
+                    in0=accs[i][0][:].rearrange("p (a q f) -> p a q f", a=2, q=2),
                     in1=table[:, j0 : j0 + 2, :].unsqueeze(2).to_broadcast([P, 2, 2, DH]),
                     op=ALU.mult,
                 )
-            nc.scalar.copy(out=ov[:, jj0 : jj0 + 2, :], in_=vv[:].rearrange("p (a f) -> p a f", a=2))
+
+        def vcopy(i):
+            c = i // 2
+            jj0 = (i % 2) * 2
+            if i % 2 == 0:
+                ov = outp.tile([P, JN, DH], F32)
+                ovs[c] = ov
+            nc.scalar.copy(
+                out=ovs[c][:, jj0 : jj0 + 2, :], in_=accs[i][1][:].rearrange("p (a f) -> p a f", a=2)
+            )
+
+        def adds(c, lo, hi, engines):
+            if lo == 0:
+                oqk = outp.tile([P, 2, JN, DH], F32)
+                oqks[c] = oqk
             for h in range(2):
-                adder = nc.vector if (i == NP - 1 and h == 0) else nc.gpsimd
-                adder.tensor_tensor(
-                    out=oqk[:, :, jj0 : jj0 + 2, h * HALF : (h + 1) * HALF],
-                    in0=pt[:, 0, :, :, h * HALF : (h + 1) * HALF].rearrange("p a q f -> p q a f"),
-                    in1=pt[:, 1, :, :, (1 - h) * HALF : (2 - h) * HALF].rearrange("p a q f -> p q a f"),
+                engines[h].tensor_tensor(
+                    out=oqks[c][:, :, lo:hi, h * HALF : (h + 1) * HALF],
+                    in0=pts[c][:, 0, lo:hi, :, h * HALF : (h + 1) * HALF].rearrange("p a q f -> p q a f"),
+                    in1=pts[c][:, 1, lo:hi, :, (1 - h) * HALF : (2 - h) * HALF].rearrange("p a q f -> p q a f"),
                     op=ALU.add,
                 )
-            if c == NCH - 1:
-                store(c, jj0, jj0 + 2)
-            elif i % 2 == 1:
-                store(c, 0, JN)
-                if c + LEAD < NCH:
-                    load(c + LEAD, 1)
 
         transposes(0)
-        regroup(0)
+        regroup_tile(0, 0)
+        for part in range(5):
+            table_scalar(0, part)
+        regroup_tile(0, 1)
         transposes(1)
         regroup(1)
-        for i in range(NP):
-            if i + 2 < NP:
-                transposes(i + 2)
-            quantise(i)
-            multiply(i)
-            if i >= 1:
-                finish(i - 1)
-            if i + 2 < NP:
-                regroup(i + 2)
-            nxt = i // 8 + 1
+        transposes(2)
+        transposes(3)
+        regroup(2)
+        regroup(3)
+        for s in range(NCH + 1):
+            i = 2 * s
+            last = s == NCH
+            if not last:
+                quantise(i)
+                quantise(i + 1)
+            if s >= 1:
+                products(i - 2)
+                if last:
+                    adds(s - 1, 0, 2, (nc.gpsimd, nc.gpsimd))
+                    store(s - 1, 0, 2)
+            if not last:
+                multiply(i)
+            if s >= 1:
+                products(i - 1)
+            if not last:
+                multiply(i + 1)
+            if i + 5 < NP:
+                transposes(i + 4)
+                transposes(i + 5)
+            if last:
+                adds(s - 1, 2, JN, (nc.vector, nc.gpsimd))
+                store(s - 1, 2, JN)
+            elif s >= 1:
+                adds(s - 1, 0, JN, (nc.gpsimd, nc.gpsimd))
+                store(s - 1, 0, JN)
+                if s - 1 + LEAD < NCH:
+                    load(s - 1 + LEAD)
+            if not last:
+                vcopy(i)
+                vcopy(i + 1)
+            if i + 5 < NP:
+                regroup(i + 4)
+                regroup(i + 5)
+            nxt = s // 4 + 1
             if nxt < J // JN:
-                if i % 8 == 2:
+                if s % 4 == 0:
+                    table_gpsimd(nxt)
+                elif s % 4 == 1:
                     table_vector(nxt)
-                if i % 8 >= 3:
-                    table_scalar(nxt, i % 8 - 3)
-        finish(NP - 1)
+                elif s % 4 == 2:
+                    for part in range(3):
+                        table_scalar(nxt, part)
+                else:
+                    for part in range(3, 5):
+                        table_scalar(nxt, part)

@@ -331,7 +331,7 @@ def tile_spikinggroupedslidingattention_pa_t_kernel(tc, x, Wq, Wk, Wv, out_0, ou
                 adds(s - 1, 2, JN, (nc.vector, nc.gpsimd))
                 store(s - 1, 2, JN)
             elif s >= 1:
-                adds(s - 1, 0, JN, (nc.gpsimd, nc.gpsimd))
+                adds(s - 1, 0, JN, (nc.gpsimd, nc.gpsimd if s % 3 == 0 else nc.vector))
                 store(s - 1, 0, JN)
                 if s - 1 + LEAD < NCH:
                     load(s - 1 + LEAD)

@@ -36,8 +36,8 @@ def tile_spikinggroupedslidingattention_pa_t_kernel(tc, x, Wq, Wk, Wv, out_0, ou
         const = ctx.enter_context(tc.tile_pool(name="const", bufs=1))
         xin = ctx.enter_context(tc.tile_pool(name="xin", bufs=NB))
         grp = ctx.enter_context(tc.tile_pool(name="grp", bufs=4))
-        cod = ctx.enter_context(tc.tile_pool(name="cod", bufs=4))
-        prod = ctx.enter_context(tc.tile_pool(name="prod", bufs=2))
+        cod = ctx.enter_context(tc.tile_pool(name="cod", bufs=3))
+        prod = ctx.enter_context(tc.tile_pool(name="prod", bufs=3))
         outp = ctx.enter_context(tc.tile_pool(name="outp", bufs=4))
         tb = ctx.enter_context(tc.tile_pool(name="tb", bufs=1))
         ps_t = ctx.enter_context(tc.psum_pool(name="ps_t", bufs=4))
@@ -110,23 +110,17 @@ def tile_spikinggroupedslidingattention_pa_t_kernel(tc, x, Wq, Wk, Wv, out_0, ou
         halves = {}
         squares = {}
 
-        def table_gpsimd(jc):
-            js = slice(jc * JN, (jc + 1) * JN)
+        def table_turns(jc):
             turns = tb.tile([P, JN, NF], F32)
-            nc.gpsimd.tensor_tensor(
-                out=turns[:],
-                in0=pos[:, js].unsqueeze(2).to_broadcast([P, JN, NF]),
-                in1=fq[:].unsqueeze(1).to_broadcast([P, JN, NF]),
-                op=ALU.mult,
-            )
-            whole = tb.tile([P, JN, NF], I32)
-            nc.gpsimd.tensor_scalar(
-                out=whole[:], in0=turns[:], scalar1=1.0, scalar2=0.0, op0=ALU.mult, op1=ALU.add
-            )
-            raws[jc] = (turns, whole)
+            for jj in range(JN):
+                j = jc * JN + jj
+                nc.scalar.activation(out=turns[:, jj, :], in_=fq[:], func=ACT.Copy, scale=pos[:, j : j + 1])
+            raws[jc] = turns
 
         def table_vector(jc):
-            turns, whole = raws[jc]
+            turns = raws[jc]
+            whole = tb.tile([P, JN, NF], I32)
+            nc.vector.tensor_copy(out=whole[:], in_=turns[:])
             frac = tb.tile([P, JN, NF], F32)
             nc.vector.tensor_tensor(out=frac[:], in0=turns[:], in1=whole[:], op=ALU.subtract)
             tabs[jc] = frac
@@ -165,7 +159,7 @@ def tile_spikinggroupedslidingattention_pa_t_kernel(tc, x, Wq, Wk, Wv, out_0, ou
                     scale=-2.0 * math.pi,
                 )
 
-        table_gpsimd(0)
+        table_turns(0)
         table_vector(0)
 
         wg = const.tile([P, 2, 3 * DH, 4], BF16, align_bytes=64)
@@ -303,53 +297,32 @@ def tile_spikinggroupedslidingattention_pa_t_kernel(tc, x, Wq, Wk, Wv, out_0, ou
         regroup_tile(0, 1)
         transposes(1)
         regroup(1)
-        transposes(2)
-        transposes(3)
-        regroup(2)
-        regroup(3)
-        for s in range(NCH + 1):
-            i = 2 * s
-            last = s == NCH
-            if not last:
+        for i in range(NP + 1):
+            if i + 2 < NP:
+                transposes(i + 2)
+            if i < NP:
                 quantise(i)
-                quantise(i + 1)
-            if s >= 1:
-                products(i - 2)
-                if last:
-                    adds(s - 1, 0, 2, (nc.gpsimd, nc.gpsimd))
-                    store(s - 1, 0, 2)
-            if not last:
                 multiply(i)
-            if s >= 1:
+            if i >= 1:
+                c = (i - 1) // 2
                 products(i - 1)
-            if not last:
-                multiply(i + 1)
-            if i + 5 < NP:
-                transposes(i + 4)
-                transposes(i + 5)
-            if last:
-                adds(s - 1, 2, JN, (nc.vector, nc.gpsimd))
-                store(s - 1, 2, JN)
-            elif s >= 1:
-                adds(s - 1, 0, JN, (nc.gpsimd, nc.gpsimd if s % 3 == 0 else nc.vector))
-                store(s - 1, 0, JN)
-                if s - 1 + LEAD < NCH:
-                    load(s - 1 + LEAD)
-            if not last:
-                vcopy(i)
-                vcopy(i + 1)
-            if i + 5 < NP:
-                regroup(i + 4)
-                regroup(i + 5)
-            nxt = s // 4 + 1
+                vcopy(i - 1)
+                if c == NCH - 1:
+                    lo = ((i - 1) % 2) * 2
+                    adds(c, lo, lo + 2, (nc.vector if lo > 0 else nc.gpsimd, nc.gpsimd))
+                    store(c, lo, lo + 2)
+                elif (i - 1) % 2 == 1:
+                    adds(c, 0, JN, (nc.gpsimd, nc.vector if c % 3 == 0 else nc.gpsimd))
+                    store(c, 0, JN)
+                    if c + LEAD < NCH:
+                        load(c + LEAD)
+            if i + 2 < NP:
+                regroup(i + 2)
+            nxt = i // 8 + 1
             if nxt < J // JN:
-                if s % 4 == 0:
-                    table_gpsimd(nxt)
-                elif s % 4 == 1:
+                if i % 8 == 0:
+                    table_turns(nxt)
+                elif i % 8 == 1:
                     table_vector(nxt)
-                elif s % 4 == 2:
-                    for part in range(3):
-                        table_scalar(nxt, part)
-                else:
-                    for part in range(3, 5):
-                        table_scalar(nxt, part)
+                elif i % 8 <= 6:
+                    table_scalar(nxt, i % 8 - 2)

@@ -115,14 +115,14 @@ def tile_spikinggroupedslidingattention_pa_t_kernel(tc, x, Wq, Wk, Wv, out_0, ou
             for jj in range(JN):
                 j = jc * JN + jj
                 nc.scalar.activation(out=turns[:, jj, :], in_=fq[:], func=ACT.Copy, scale=pos[:, j : j + 1])
-            raws[jc] = turns
+            whole = tb.tile([P, JN, NF], U32)
+            nc.scalar.copy(out=whole[:], in_=turns[:])
+            raws[jc] = (turns, whole)
 
         def table_vector(jc):
-            turns = raws[jc]
-            whole = tb.tile([P, JN, NF], I32)
-            nc.vector.tensor_copy(out=whole[:], in_=turns[:])
+            turns, whole = raws[jc]
             frac = tb.tile([P, JN, NF], F32)
-            nc.vector.tensor_tensor(out=frac[:], in0=turns[:], in1=whole[:], op=ALU.subtract)
+            nc.vector.tensor_tensor(out=frac[:], in0=turns[:], in1=whole[:].bitcast(I32), op=ALU.subtract)
             tabs[jc] = frac
 
         def table_scalar(jc, part):
@@ -258,11 +258,11 @@ def tile_spikinggroupedslidingattention_pa_t_kernel(tc, x, Wq, Wk, Wv, out_0, ou
             jj0 = (i % 2) * 2
             j0 = jc * JN + jj0
             if i % 2 == 0:
-                pt = prod.tile([P, 2, JN, 2, DH], F32)
+                pt = prod.tile([P, 2, 2, JN, DH], F32)
                 pts[c] = pt
             for k, table in enumerate((cos_t, sin_t)):
                 nc.vector.tensor_tensor(
-                    out=pts[c][:, k, jj0 : jj0 + 2, :, :],
+                    out=pts[c][:, k, :, jj0 : jj0 + 2, :].rearrange("p q a f -> p a q f"),
                     in0=accs[i][0][:].rearrange("p (a q f) -> p a q f", a=2, q=2),
                     in1=table[:, j0 : j0 + 2, :].unsqueeze(2).to_broadcast([P, 2, 2, DH]),
                     op=ALU.mult,
@@ -285,8 +285,8 @@ def tile_spikinggroupedslidingattention_pa_t_kernel(tc, x, Wq, Wk, Wv, out_0, ou
             for h in range(2):
                 engines[h].tensor_tensor(
                     out=oqks[c][:, :, lo:hi, h * HALF : (h + 1) * HALF],
-                    in0=pts[c][:, 0, lo:hi, :, h * HALF : (h + 1) * HALF].rearrange("p a q f -> p q a f"),
-                    in1=pts[c][:, 1, lo:hi, :, (1 - h) * HALF : (2 - h) * HALF].rearrange("p a q f -> p q a f"),
+                    in0=pts[c][:, 0, :, lo:hi, h * HALF : (h + 1) * HALF],
+                    in1=pts[c][:, 1, :, lo:hi, (1 - h) * HALF : (2 - h) * HALF],
                     op=ALU.add,
                 )
 
@@ -312,7 +312,7 @@ def tile_spikinggroupedslidingattention_pa_t_kernel(tc, x, Wq, Wk, Wv, out_0, ou
                     adds(c, lo, lo + 2, (nc.vector if lo > 0 else nc.gpsimd, nc.gpsimd))
                     store(c, lo, lo + 2)
                 elif (i - 1) % 2 == 1:
-                    adds(c, 0, JN, (nc.gpsimd, nc.vector if c % 3 == 0 else nc.gpsimd))
+                    adds(c, 0, JN, (nc.gpsimd, nc.vector if c % 2 == 0 else nc.gpsimd))
                     store(c, 0, JN)
                     if c + LEAD < NCH:
                         load(c + LEAD)

@@ -216,18 +216,25 @@ def tile_spikinggroupedslidingattention_pa_t_kernel(tc, x, Wq, Wk, Wv, out_0, ou
         def quantise(i):
             xcod = cod.tile([P, D // 2], U32, align_bytes=64)
             xsc = cod.tile([P, D // 2], U8, align_bytes=64)
-            nc.vector.quantize_mx(out=xcod[:].bitcast(FP8X4), scales=xsc[:], in_=grs[i][:])
+            for a in range(2):
+                nc.vector.quantize_mx(
+                    out=xcod[:, a * (D // 4) : (a + 1) * (D // 4)].bitcast(FP8X4),
+                    scales=xsc[:, a * (D // 4) : (a + 1) * (D // 4)],
+                    in_=grs[i][:, a * D : (a + 1) * D],
+                )
             cods[i] = (xcod, xsc)
 
         def multiply(i):
             xcod, xsc = cods[i]
             qk = ps_q.tile([P, 4 * DH], F32)
             vv = ps_v.tile([P, 2 * DH], F32)
-            for a in range(2):
-                for dst, c0, c1 in (
-                    (qk[:, a * 2 * DH : (a + 1) * 2 * DH], 0, 2 * DH),
-                    (vv[:, a * DH : (a + 1) * DH], 2 * DH, 3 * DH),
-                ):
+            for a, dst, c0, c1 in (
+                (0, qk[:, 0 : 2 * DH], 0, 2 * DH),
+                (1, qk[:, 2 * DH : 4 * DH], 0, 2 * DH),
+                (0, vv[:, 0:DH], 2 * DH, 3 * DH),
+                (1, vv[:, DH : 2 * DH], 2 * DH, 3 * DH),
+            ):
+                if True:
                     for g in range(2):
                         cols = slice((a * 2 + g) * P, (a * 2 + g + 1) * P)
                         nc.tensor.matmul_mx(

@@ -43,7 +43,6 @@ def tile_spikinggroupedslidingattention_pa_t_kernel(tc, x, Wq, Wk, Wv, out_0, ou
         ps_t = ctx.enter_context(tc.psum_pool(name="ps_t", bufs=4))
         ps_q = ctx.enter_context(tc.psum_pool(name="ps_q", bufs=2))
         ps_v = ctx.enter_context(tc.psum_pool(name="ps_v", bufs=2))
-        ctx.enter_context(tc.manual_schedule())
 
         xcs = {}
         xts = {}
@@ -216,25 +215,18 @@ def tile_spikinggroupedslidingattention_pa_t_kernel(tc, x, Wq, Wk, Wv, out_0, ou
         def quantise(i):
             xcod = cod.tile([P, D // 2], U32, align_bytes=64)
             xsc = cod.tile([P, D // 2], U8, align_bytes=64)
-            for a in range(2):
-                nc.vector.quantize_mx(
-                    out=xcod[:, a * (D // 4) : (a + 1) * (D // 4)].bitcast(FP8X4),
-                    scales=xsc[:, a * (D // 4) : (a + 1) * (D // 4)],
-                    in_=grs[i][:, a * D : (a + 1) * D],
-                )
+            nc.vector.quantize_mx(out=xcod[:].bitcast(FP8X4), scales=xsc[:], in_=grs[i][:])
             cods[i] = (xcod, xsc)
 
         def multiply(i):
             xcod, xsc = cods[i]
             qk = ps_q.tile([P, 4 * DH], F32)
             vv = ps_v.tile([P, 2 * DH], F32)
-            for a, dst, c0, c1 in (
-                (0, qk[:, 0 : 2 * DH], 0, 2 * DH),
-                (1, qk[:, 2 * DH : 4 * DH], 0, 2 * DH),
-                (0, vv[:, 0:DH], 2 * DH, 3 * DH),
-                (1, vv[:, DH : 2 * DH], 2 * DH, 3 * DH),
-            ):
-                if True:
+            for a in range(2):
+                for dst, c0, c1 in (
+                    (qk[:, a * 2 * DH : (a + 1) * 2 * DH], 0, 2 * DH),
+                    (vv[:, a * DH : (a + 1) * DH], 2 * DH, 3 * DH),
+                ):
                     for g in range(2):
                         cols = slice((a * 2 + g) * P, (a * 2 + g + 1) * P)
                         nc.tensor.matmul_mx(

import math
from contextlib import ExitStack

import concourse.mybir as mybir
from concourse.masks import make_identity

F32 = mybir.dt.float32
BF16 = mybir.dt.bfloat16
I32 = mybir.dt.int32
U32 = mybir.dt.uint32
U8 = mybir.dt.uint8
FP8X4 = mybir.dt.float8_e4m3fn_x4
ALU = mybir.AluOpType
ACT = mybir.ActivationFunctionType

B, S, D, DH = 4, 2048, 1024, 128
THETA = 10000.0
P = 128
J = S // P
JN = 4
NCH = B * J // JN
NP = NCH * JN // 2
LEAD = 8
NB = 10
HALF = DH // 2
NF = DH // 2
NSEED = 8

FLOPS = 2 * B * S * D * 3 * DH


def tile_spikinggroupedslidingattention_pa_t_kernel(tc, x, Wq, Wk, Wv, out_0, out_1, out_2):
    nc = tc.nc
    chunks = [(jc, b) for jc in range(J // JN) for b in range(B)]
    with ExitStack() as ctx:
        const = ctx.enter_context(tc.tile_pool(name="const", bufs=1))
        xin = ctx.enter_context(tc.tile_pool(name="xin", bufs=NB))
        grp = ctx.enter_context(tc.tile_pool(name="grp", bufs=4))
        cod = ctx.enter_context(tc.tile_pool(name="cod", bufs=3))
        prod = ctx.enter_context(tc.tile_pool(name="prod", bufs=3))
        outp = ctx.enter_context(tc.tile_pool(name="outp", bufs=4))
        tb = ctx.enter_context(tc.tile_pool(name="tb", bufs=1))
        ps_t = ctx.enter_context(tc.psum_pool(name="ps_t", bufs=4))
        ps_q = ctx.enter_context(tc.psum_pool(name="ps_q", bufs=2))
        ps_v = ctx.enter_context(tc.psum_pool(name="ps_v", bufs=2))

        xcs = {}
        xts = {}
        grs = {}
        cods = {}
        accs = {}
        oqks = {}
        pts = {}
        ovs = {}

        def load_part(c, lo, hi):
            jc, b = chunks[c]
            nc.sync.dma_start(
                out=xcs[c][:, lo * D : hi * D].rearrange("p (j d) -> p j d", j=hi - lo),
                in_=x[b].rearrange("(p j) d -> p j d", j=J)[:, jc * JN + lo : jc * JN + hi, :],
            )

        def load(c):
            xc = xin.tile([P, JN * D], BF16)
            xcs[c] = xc
            if c > 0:
                load_part(c, 0, JN)

        wraw = const.tile([P, 3, 2, 4, DH], BF16)
        load(0)
        load_part(0, 0, 1)
        for wi, w_dram in enumerate((Wq, Wk, Wv)):
            nc.sync.dma_start(
                out=wraw[:, wi].rearrange("p g (u e) n -> p (g u) (e n)", u=2, e=2),
                in_=w_dram.rearrange("(a w e) n -> w a (e n)", a=4, w=P, e=2),
            )
        load_part(0, 1, 2)
        load_part(0, 2, JN)
        for c in range(1, LEAD):
            load(c)

        ident = const.tile([P, P], F32)
        make_identity(nc, ident[:])
        pos_i = const.tile([P, J], I32)
        nc.gpsimd.iota(pos_i[:], pattern=[[1, J]], base=0, channel_multiplier=J)

        ones = const.tile([P, NSEED], F32)
        nc.vector.memset(ones[:], 1.0)
        warm = const.tile([P, 1], F32)
        nc.scalar.activation(out=warm[:], in_=ones[:, 0:1], func=ACT.Sin)
        fq = const.tile([P, NF], F32)
        for m in range(NSEED):
            nc.vector.tensor_scalar_mul(
                out=fq[:, m : m + 1], in0=ones[:, m : m + 1], scalar1=THETA ** (-m / NF) / (2.0 * math.pi)
            )
        n_have = NSEED
        while n_have < NF:
            nc.vector.tensor_scalar_mul(
                out=fq[:, n_have : 2 * n_have], in0=fq[:, 0:n_have], scalar1=THETA ** (-n_have / NF)
            )
            n_have *= 2
        pos = const.tile([P, J], F32)
        nc.vector.tensor_copy(out=pos[:], in_=pos_i[:])

        cos_t = const.tile([P, J, DH], F32)
        sin_t = const.tile([P, J, DH], F32)
        tabs = {}
        raws = {}
        halves = {}
        squares = {}

        def table_turns(jc):
            turns = tb.tile([P, JN, NF], F32)
            for jj in range(JN):
                j = jc * JN + jj
                nc.scalar.activation(out=turns[:, jj, :], in_=fq[:], func=ACT.Copy, scale=pos[:, j : j + 1])
            whole = tb.tile([P, JN, NF], U32)
            nc.scalar.copy(out=whole[:], in_=turns[:])
            raws[jc] = (turns, whole)

        def table_vector(jc):
            turns, whole = raws[jc]
            frac = tb.tile([P, JN, NF], F32)
            nc.vector.tensor_tensor(out=frac[:], in0=turns[:], in1=whole[:].bitcast(I32), op=ALU.subtract)
            tabs[jc] = frac

        def table_scalar(jc, part):
            js = slice(jc * JN, (jc + 1) * JN)
            frac = tabs[jc]
            if part == 0:
                hs = tb.tile([P, JN, NF], F32)
                nc.scalar.activation(out=hs[:], in_=frac[:], func=ACT.Sin, scale=math.pi)
                halves[jc] = hs
            elif part == 1:
                sq = tb.tile([P, JN, NF], F32)
                nc.scalar.activation(out=sq[:], in_=halves[jc][:], func=ACT.Square)
                squares[jc] = sq
            elif part == 2:
                nc.scalar.activation(
                    out=cos_t[:, js, :].rearrange("p j (m e) -> p j m e", e=2),
                    in_=squares[jc][:].unsqueeze(3).to_broadcast([P, JN, NF, 2]),
                    func=ACT.Copy,
                    bias=1.0,
                    scale=-2.0,
                )
            elif part == 3:
                nc.scalar.activation(
                    out=sin_t[:, js, 0:HALF].rearrange("p j (m e) -> p j m e", e=2),
                    in_=frac[:, :, NF // 2 : NF].unsqueeze(3).to_broadcast([P, JN, NF // 2, 2]),
                    func=ACT.Sin,
                    scale=2.0 * math.pi,
                )
            else:
                nc.scalar.activation(
                    out=sin_t[:, js, HALF:DH].rearrange("p j (m e) -> p j m e", e=2),
                    in_=frac[:, :, 0 : NF // 2].unsqueeze(3).to_broadcast([P, JN, NF // 2, 2]),
                    func=ACT.Sin,
                    scale=-2.0 * math.pi,
                )

        table_turns(0)
        table_vector(0)

        wg = const.tile([P, 2, 3 * DH, 4], BF16, align_bytes=64)
        for wi in range(3):
            if wi < 2:
                nc.vector.tensor_copy(
                    out=wg[:, :, wi * DH : (wi + 1) * DH, :], in_=wraw[:, wi].rearrange("p g t n -> p g n t")
                )
            else:
                nc.gpsimd.tensor_scalar(
                    out=wg[:, :, wi * DH : (wi + 1) * DH, :],
                    in0=wraw[:, wi].rearrange("p g t n -> p g n t"),
                    scalar1=1.0,
                    scalar2=0.0,
                    op0=ALU.mult,
                    op1=ALU.add,
                )
        wcod = const.tile([P, 2, 3 * DH], U32, align_bytes=64)
        wsc = const.tile([P, 2, 3 * DH], U8, align_bytes=64)
        for c0, c1 in ((0, 2 * DH), (2 * DH, 3 * DH)):
            for g in range(2):
                nc.vector.quantize_mx(
                    out=wcod[:, g, c0:c1].bitcast(FP8X4),
                    scales=wsc[:, g, c0:c1],
                    in_=wg[:, g, c0:c1, :].rearrange("p n t -> p (n t)"),
                )

        def transposes(i):
            xw = xcs[i // 2][:].bitcast(F32)
            tiles = []
            for a in range(2):
                jj = (i % 2) * 2 + a
                xt = ps_t.tile([P, 4, P], F32)
                for u in range(4):
                    col = jj * (D // 2) + u * P
                    nc.tensor.transpose(xt[:, u, :], xw[:, col : col + P], ident[:])
                tiles.append(xt)
            xts[i] = tiles

        def regroup_tile(i, a):
            if a == 0:
                gr = grp.tile([P, 2 * D], BF16, align_bytes=64)
                grs[i] = gr
            grw = grs[i][:].bitcast(F32)
            nc.scalar.copy(
                out=grw[:, a * (D // 2) : (a + 1) * (D // 2)].rearrange("p (g r u) -> p g r u", g=2, r=P, u=2),
                in_=xts[i][a][:].rearrange("p (g u) r -> p g r u", g=2, u=2),
            )

        def regroup(i):
            regroup_tile(i, 0)
            regroup_tile(i, 1)

        def quantise(i):
            xcod = cod.tile([P, D // 2], U32, align_bytes=64)
            xsc = cod.tile([P, D // 2], U8, align_bytes=64)
            nc.vector.quantize_mx(out=xcod[:].bitcast(FP8X4), scales=xsc[:], in_=grs[i][:])
            cods[i] = (xcod, xsc)

        def multiply(i):
            xcod, xsc = cods[i]
            qk = ps_q.tile([P, 4 * DH], F32)
            vv = ps_v.tile([P, 2 * DH], F32)
            for a in range(2):
                for dst, c0, c1 in (
                    (qk[:, a * 2 * DH : (a + 1) * 2 * DH], 0, 2 * DH),
                    (vv[:, a * DH : (a + 1) * DH], 2 * DH, 3 * DH),
                ):
                    for g in range(2):
                        cols = slice((a * 2 + g) * P, (a * 2 + g + 1) * P)
                        nc.tensor.matmul_mx(
                            out=dst,
                            lhsT=xcod[:, cols].bitcast(FP8X4),
                            lhsT_scale=xsc[:, cols],
                            rhs=wcod[:, g, c0:c1].bitcast(FP8X4),
                            rhs_scale=wsc[:, g, c0:c1],
                            start=(g == 0),
                            stop=(g == 1),
                        )
            accs[i] = (qk, vv)

        def store(c, lo, hi):
            jc, b = chunks[c]
            js = slice(jc * JN + lo, jc * JN + hi)
            oqk = oqks[c]
            for dram, src in (
                (out_0, oqk[:, 0, lo:hi, :]),
                (out_1, oqk[:, 1, lo:hi, :]),
                (out_2, ovs[c][:, lo:hi, :]),
            ):
                nc.sync.dma_start(out=dram[b, 0].rearrange("(p j) f -> p j f", j=J)[:, js, :], in_=src)

        def products(i):
            c = i // 2
            jc, b = chunks[c]
            jj0 = (i % 2) * 2
            j0 = jc * JN + jj0
            if i % 2 == 0:
                pt = prod.tile([P, 2, 2, JN, DH], F32)
                pts[c] = pt
            for k, table in enumerate((cos_t, sin_t)):
                nc.vector.tensor_tensor(
                    out=pts[c][:, k, :, jj0 : jj0 + 2, :].rearrange("p q a f -> p a q f"),
                    in0=accs[i][0][:].rearrange("p (a q f) -> p a q f", a=2, q=2),
                    in1=table[:, j0 : j0 + 2, :].unsqueeze(2).to_broadcast([P, 2, 2, DH]),
                    op=ALU.mult,
                )

        def vcopy(i):
            c = i // 2
            jj0 = (i % 2) * 2
            if i % 2 == 0:
                ov = outp.tile([P, JN, DH], F32)
                ovs[c] = ov
            nc.scalar.copy(
                out=ovs[c][:, jj0 : jj0 + 2, :], in_=accs[i][1][:].rearrange("p (a f) -> p a f", a=2)
            )

        def adds(c, lo, hi, engines):
            if lo == 0:
                oqk = outp.tile([P, 2, JN, DH], F32)
                oqks[c] = oqk
            for h in range(2):
                engines[h].tensor_tensor(
                    out=oqks[c][:, :, lo:hi, h * HALF : (h + 1) * HALF],
                    in0=pts[c][:, 0, :, lo:hi, h * HALF : (h + 1) * HALF],
                    in1=pts[c][:, 1, :, lo:hi, (1 - h) * HALF : (2 - h) * HALF],
                    op=ALU.add,
                )

        transposes(0)
        regroup_tile(0, 0)
        for part in range(5):
            table_scalar(0, part)
        regroup_tile(0, 1)
        transposes(1)
        regroup(1)
        for i in range(NP + 1):
            if i + 2 < NP:
                transposes(i + 2)
            if i < NP:
                quantise(i)
                multiply(i)
            if i >= 1:
                c = (i - 1) // 2
                products(i - 1)
                vcopy(i - 1)
                if c == NCH - 1:
                    lo = ((i - 1) % 2) * 2
                    adds(c, lo, lo + 2, (nc.vector if lo > 0 else nc.gpsimd, nc.gpsimd))
                    store(c, lo, lo + 2)
                elif (i - 1) % 2 == 1:
                    adds(c, 0, JN, (nc.gpsimd, nc.vector if c % 2 == 0 else nc.gpsimd))
                    store(c, 0, JN)
                    if c + LEAD < NCH:
                        load(c + LEAD)
            if i + 2 < NP:
                regroup(i + 2)
            nxt = i // 8 + 1
            if nxt < J // JN:
                if i % 8 == 0:
                    table_turns(nxt)
                elif i % 8 == 1:
                    table_vector(nxt)
                elif i % 8 <= 6:
                    table_scalar(nxt, i % 8 - 2)
